import numpy as np
import ml_dtypes


def mxq(x, axis, fmt="e4m3"):
    dtype, down = {"e4m3": (ml_dtypes.float8_e4m3fn, 7), "e5m2": (ml_dtypes.float8_e5m2, 14)}[fmt]
    v = np.moveaxis(np.asarray(x, np.float32).astype(ml_dtypes.bfloat16).astype(np.float64), axis, -1)
    blocks = v.reshape(v.shape[:-1] + (-1, 32))
    amax = np.abs(blocks).max(-1, keepdims=True)
    byte = np.maximum(np.where(amax > 0, np.frexp(amax)[1] - 1 + 127, 0) - down, 1)
    scale = np.exp2(byte - 127.0)
    codes = (blocks / scale).astype(np.float32).astype(dtype).astype(np.float64)
    return np.moveaxis((codes * scale).reshape(v.shape), -1, axis)


WIDE = False


def mx_kscale(k):
    if not WIDE:
        return np.ones(k)
    levels = np.array([10, -10, 5, -5, 0])
    a = np.random.permutation(np.resize(levels, k // 512 * 4)).reshape(k // 512, 4)
    idx = np.arange(k)
    return np.exp2(a[idx // 512, idx % 128 // 32])


BF16 = ml_dtypes.bfloat16


def bf(x):
    return np.asarray(x, np.float32).astype(BF16)


def f64(x):
    return np.asarray(x).astype(np.float64)


B, T, N, C = 4, 4, 512, 512
EDGE = 0.0625


def sigmoid(z):
    return 1.0 / (1.0 + np.exp(-z))


def setup_inputs():
    s = mx_kscale(C)
    return {"x": bf(np.random.standard_normal((B, T, N, C)) * 0.5),
            "hid": bf(np.maximum(np.random.standard_normal((B, T, N, C)), 0.0) * s),
            "adj": bf(np.random.random((B, N, N)) * (np.random.random((B, N, N)) < EDGE)),
            "lam_raw": bf(3.5 + 0.1 * np.random.standard_normal(1)),
            "theta": bf(np.random.standard_normal((C, C)) * 4.5 / np.sqrt(C) / s[:, None])}


def reference(x, hid, adj, lam_raw, theta):
    lam = 1.0 + np.maximum(f64(lam_raw)[0], 0.0)
    h = mxq(f64(hid), 3, "e4m3") @ mxq(f64(theta), 0, "e4m3")
    v = ((2.0 * lam - 2.0) / lam) * np.eye(N) + (2.0 / lam) * f64(adj)
    v = v / np.sum(v, axis=-1, keepdims=True)
    out = mxq(v, 2, "e4m3")[:, None] @ mxq(h, 2, "e4m3")
    return np.maximum(f64(x), 0.0) + sigmoid(np.maximum(out, 0.0))

@@ -1,0 +1,265 @@
+from contextlib import ExitStack
+
+import concourse.mybir as mybir
+from concourse.masks import make_identity
+
+F32 = mybir.dt.float32
+BF16 = mybir.dt.bfloat16
+U32 = mybir.dt.uint32
+U8 = mybir.dt.uint8
+FP8X4 = mybir.dt.float8_e4m3fn_x4
+ALU = mybir.AluOpType
+ACT = mybir.ActivationFunctionType
+
+B, T, N, C = 4, 4, 512, 512
+P = 128
+NJ = B * T
+FLOPS = 2 * B * T * N * C * C + 2 * B * T * N * N * C
+DIAG = 513
+VW = 2112
+
+
+def tile_akgcn_pb_t_kernel(tc, x, hid, adj, lam_raw, theta, out):
+    nc = tc.nc
+    with ExitStack() as ctx:
+        const = ctx.enter_context(tc.tile_pool(name="const", bufs=1))
+        hid_pool = ctx.enter_context(tc.tile_pool(name="hid_pool", bufs=5))
+        x_pool = ctx.enter_context(tc.tile_pool(name="x_pool", bufs=6))
+        o_pool = ctx.enter_context(tc.tile_pool(name="o_pool", bufs=4))
+        g_pool = ctx.enter_context(tc.tile_pool(name="g_pool", bufs=2))
+        c_pool = ctx.enter_context(tc.tile_pool(name="c_pool", bufs=3))
+        v_pool = ctx.enter_context(tc.tile_pool(name="v_pool", bufs=2))
+        tp_pool = ctx.enter_context(tc.psum_pool(name="tp_pool", bufs=2))
+        h_pool = ctx.enter_context(tc.psum_pool(name="h_pool", bufs=3))
+        z_pool = ctx.enter_context(tc.psum_pool(name="z_pool", bufs=3))
+
+        hid_t, x_t, adj_t = {}, {}, {}
+        hid_g, hid_q, h_g, h_q, v_q = {}, {}, {}, {}, {}
+        a_g, r_ps = {}, {}
+        count = {"tp": 0}
+
+        def evacuate(engine, dst, src):
+            if engine == "s":
+                nc.scalar.copy(out=dst, in_=src)
+            else:
+                nc.vector.tensor_copy(out=dst, in_=src)
+
+        def quantise(src, name):
+            codes = c_pool.tile([P, 512], U32, name=name + "_c", align_bytes=64)
+            scales = c_pool.tile([P, 512], U8, name=name + "_s", align_bytes=64)
+            nc.vector.quantize_mx(out=codes[:].bitcast(FP8X4), scales=scales[:], in_=src)
+            return codes, scales
+
+        def load_hid(j):
+            hid_t[j] = hid_pool.tile([P, 4 * C], BF16, name="hid_t")
+            nc.sync.dma_start(out=hid_t[j][:], in_=hid[j // T, j % T].rearrange("(p t) c -> p (t c)", t=4))
+
+        def load_x(j):
+            x_t[j] = x_pool.tile([P, 4 * C], BF16, name="x_t")
+            nc.sync.dma_start(out=x_t[j][:], in_=x[j // T, j % T].rearrange("(p i) c -> p (i c)", i=4))
+
+        def load_adj(b):
+            adj_t[b] = v_pool.tile([P, 4 * N], BF16, name="adj_t")
+            nc.sync.dma_start(out=adj_t[b][:], in_=adj[b].rearrange("(p i) m -> p (i m)", i=4))
+
+        def word_transposes(words, step, dst_words, engines):
+            for half in range(2):
+                tp = tp_pool.tile([P, 2, 2, P], F32, name="tp")
+                for lo in range(2):
+                    for u in range(2):
+                        base = (2 * half + lo) * 256
+                        if step == 1:
+                            src = words[:, base + u * P : base + (u + 1) * P]
+                        else:
+                            src = words[:, base + u : base + 256 : 2]
+                        nc.tensor.transpose(tp[:, lo, u, :], src, ident[:])
+                evacuate(
+                    engines[half],
+                    dst_words[:, half * 512 : (half + 1) * 512].rearrange("q (l p u) -> q l p u", l=2, u=2),
+                    tp[:].rearrange("q l u p -> q l p u"),
+                )
+
+        def stage_t(j):
+            hid_g[j] = g_pool.tile([P, 4 * N], BF16, name="hid_g", align_bytes=64)
+            engines = []
+            for half in range(2):
+                engines.append("v" if count["tp"] % 3 == 2 else "s")
+                count["tp"] += 1
+            word_transposes(hid_t[j][:].bitcast(F32), 1, hid_g[j][:].bitcast(F32), engines)
+
+        def stage_q1(j):
+            hid_q[j] = quantise(hid_g[j][:], "hid")
+
+        def stage_m1(j):
+            codes, scales = hid_q[j]
+            h_g[j] = g_pool.tile([P, C, 4], BF16, name="h_g", align_bytes=64)
+            for s in range(4):
+                cols = slice(s * P, (s + 1) * P)
+                h_ps = h_pool.tile([P, 4, P], F32, name="h_ps")
+                for t in range(4):
+                    rows = slice(t * P, (t + 1) * P)
+                    nc.tensor.matmul_mx(
+                        out=h_ps[:, t, :],
+                        lhsT=codes[:, rows].bitcast(FP8X4),
+                        lhsT_scale=scales[:, rows],
+                        rhs=th_c[:, cols].bitcast(FP8X4),
+                        rhs_scale=th_s[:, cols],
+                        start=True,
+                        stop=True,
+                    )
+                evacuate("s", h_g[j][:, cols, :], h_ps[:].rearrange("p t c -> p c t"))
+
+        def stage_q2(j):
+            h_q[j] = quantise(h_g[j][:].rearrange("p c t -> p (c t)"), "h")
+
+        def stage_m2(j, o_t):
+            codes, scales = h_q[j]
+            vc, vs = v_q[j // T]
+            for i in range(4):
+                rows = slice(i * P, (i + 1) * P)
+                z_ps = z_pool.tile([P, C], F32, name="z_ps", tag="z")
+                nc.tensor.matmul_mx(
+                    out=z_ps[:],
+                    lhsT=vc[:, rows].bitcast(FP8X4),
+                    lhsT_scale=vs[:, rows],
+                    rhs=codes[:].bitcast(FP8X4),
+                    rhs_scale=scales[:],
+                    start=True,
+                    stop=True,
+                )
+                nc.scalar.activation(out=o_t[:, i * C : (i + 1) * C], in_=z_ps[:], func=ACT.Sigmoid)
+
+        def relu_x(j):
+            nc.vector.tensor_scalar_max(out=x_t[j][:], in0=x_t[j][:], scalar1=0.0)
+
+        def finish(j, o_t, pieces):
+            dst = out[j // T, j % T].rearrange("(p i) c -> p (i c)", i=4)
+            width = 4 * C // pieces
+            for k in range(pieces):
+                cols = slice(k * width, (k + 1) * width)
+                nc.vector.scalar_tensor_tensor(
+                    out=o_t[:, cols], in0=o_t[:, cols], scalar=0.5, in1=x_t[j][:, cols], op0=ALU.max, op1=ALU.add
+                )
+                nc.sync.dma_start(out=dst[:, cols], in_=o_t[:, cols])
+
+        def v_transposes(b):
+            a_g[b] = v_pool.tile([P, VW], BF16, name="a_g", align_bytes=64)
+            word_transposes(adj_t[b][:].bitcast(F32), 2, a_g[b][:, 0 : 4 * N].bitcast(F32), ["s", "s"])
+
+        def v_sums(b):
+            grouped = a_g[b][:, 0 : 4 * N].rearrange("p (n t) -> p n t", t=4)
+            rs_ps = z_pool.tile([P, 4, 32], F32, name="rs_ps", tag="z")
+            for i in range(4):
+                for t in range(4):
+                    nc.tensor.matmul(
+                        out=rs_ps[:, i, :],
+                        lhsT=grouped[:, i * P : (i + 1) * P, t],
+                        rhs=ones[:],
+                        start=(t == 0),
+                        stop=(t == 3),
+                    )
+            s4 = v_pool.tile([P, 4], F32, name="s4")
+            nc.vector.tensor_scalar(out=s4[:], in0=rs_ps[:, :, 0], scalar1=gain[:, 0:1], scalar2=None, op0=ALU.add)
+            r4 = v_pool.tile([P, 4], F32, name="r4")
+            nc.vector.reciprocal(out=r4[:], in_=s4[:])
+            r_ps[b] = z_pool.tile([P, 4, P], F32, name="r_ps", tag="z")
+            for i in range(4):
+                nc.tensor.matmul(
+                    out=r_ps[b][:, i, :],
+                    lhsT=r4[:, i : i + 1].to_broadcast([P, P]),
+                    rhs=ident[:],
+                    start=True,
+                    stop=True,
+                )
+
+        def v_scale(b):
+            v_g = v_pool.tile([P, VW], BF16, name="v_g", align_bytes=64)
+            nc.vector.tensor_tensor(
+                out=v_g[:, 0 : 4 * N].rearrange("p (n t) -> p n t", t=4),
+                in0=a_g[b][:, 0 : 4 * N].rearrange("p (n t) -> p n t", t=4),
+                in1=r_ps[b][:].rearrange("p i n -> p (i n)").unsqueeze(2).to_broadcast([P, N, 4]),
+                op=ALU.mult,
+            )
+            w_d = v_pool.tile([P, 4, P], F32, name="w_d")
+            nc.vector.scalar_tensor_tensor(
+                out=w_d[:],
+                in0=ident[:].unsqueeze(1).to_broadcast([P, 4, P]),
+                scalar=gain[:, 0:1],
+                in1=a_g[b][:, 0 : 4 * DIAG].rearrange("p (a c) -> p a c", c=DIAG)[:, :, 0:512:4],
+                op0=ALU.mult,
+                op1=ALU.add,
+            )
+            nc.vector.tensor_tensor(
+                out=v_g[:, 0 : 4 * DIAG].rearrange("p (a c) -> p a c", c=DIAG)[:, :, 0:512:4],
+                in0=w_d[:],
+                in1=r_ps[b][:],
+                op=ALU.mult,
+            )
+            v_q[b] = quantise(v_g[:, 0 : 4 * N], "v")
+
+        th_raw = const.tile([P, 4, C], BF16, name="th_raw")
+        nc.sync.dma_start(
+            out=th_raw[:].rearrange("q (u e) n -> q u (e n)", u=2),
+            in_=theta.rearrange("(u q e) n -> q u (e n)", u=2, e=2),
+        )
+        load_hid(0)
+        load_adj(0)
+        lam_b = const.tile([P, 1], BF16, name="lam_b")
+        nc.sync.dma_start(out=lam_b[:], in_=lam_raw.partition_broadcast(P))
+        load_hid(1)
+        load_x(0)
+        load_hid(2)
+        load_x(1)
+        load_hid(3)
+
+        ident = const.tile([P, P], F32, name="ident")
+        make_identity(nc, ident[:])
+        ones = const.tile([P, 32], BF16, name="ones")
+        nc.vector.memset(ones[:], 1.0)
+        gain = const.tile([P, 1], F32, name="gain")
+        nc.vector.tensor_scalar_max(out=gain[:], in0=lam_b[:], scalar1=0.0)
+
+        th_g = const.tile([P, C, 4], BF16, name="th_g", align_bytes=64)
+        nc.vector.tensor_copy(out=th_g[:], in_=th_raw[:].rearrange("q t n -> q n t"))
+        th_c = const.tile([P, C], U32, name="th_c", align_bytes=64)
+        th_s = const.tile([P, C], U8, name="th_s", align_bytes=64)
+
+        stage_t(0)
+        nc.vector.quantize_mx(
+            out=th_c[:].bitcast(FP8X4), scales=th_s[:], in_=th_g[:].rearrange("q n t -> q (n t)")
+        )
+        v_transposes(0)
+        stage_q1(0)
+        stage_t(1)
+        stage_m1(0)
+        v_sums(0)
+        stage_q1(1)
+        v_scale(0)
+        stage_q2(0)
+
+        for k in range(NJ):
+            b, t = k // T, k % T
+            if k + 4 < NJ:
+                load_hid(k + 4)
+            if k + 2 < NJ:
+                load_x(k + 2)
+            if t == 0 and b + 1 < B:
+                load_adj(b + 1)
+            if k + 2 < NJ:
+                stage_t(k + 2)
+            if t == 1 and b + 1 < B:
+                v_transposes(b + 1)
+            if k + 1 < NJ:
+                stage_m1(k + 1)
+            o_t = o_pool.tile([P, 4 * C], F32, name="o_t")
+            stage_m2(k, o_t)
+            if t == 1 and b + 1 < B:
+                v_sums(b + 1)
+            relu_x(k)
+            if k + 2 < NJ:
+                stage_q1(k + 2)
+            finish(k, o_t, 4 if k == NJ - 1 else 1)
+            if k + 1 < NJ:
+                stage_q2(k + 1)
+            if t == 2 and b + 1 < B:
+                v_scale(b + 1)

@@ -19,12 +19,18 @@ DIAG = 513
 VW = 2112
 
 
+LEAD_T = 5
+LEAD_Q = 4
+LEAD_M = 3
+FIRST = -5
+
+
 def tile_akgcn_pb_t_kernel(tc, x, hid, adj, lam_raw, theta, out):
     nc = tc.nc
     with ExitStack() as ctx:
         const = ctx.enter_context(tc.tile_pool(name="const", bufs=1))
-        hid_pool = ctx.enter_context(tc.tile_pool(name="hid_pool", bufs=5))
-        x_pool = ctx.enter_context(tc.tile_pool(name="x_pool", bufs=6))
+        hid_pool = ctx.enter_context(tc.tile_pool(name="hid_pool", bufs=4))
+        x_pool = ctx.enter_context(tc.tile_pool(name="x_pool", bufs=5))
         o_pool = ctx.enter_context(tc.tile_pool(name="o_pool", bufs=4))
         g_pool = ctx.enter_context(tc.tile_pool(name="g_pool", bufs=2))
         c_pool = ctx.enter_context(tc.tile_pool(name="c_pool", bufs=3))
@@ -32,11 +38,11 @@ def tile_akgcn_pb_t_kernel(tc, x, hid, adj, lam_raw, theta, out):
         tp_pool = ctx.enter_context(tc.psum_pool(name="tp_pool", bufs=2))
         h_pool = ctx.enter_context(tc.psum_pool(name="h_pool", bufs=3))
         z_pool = ctx.enter_context(tc.psum_pool(name="z_pool", bufs=3))
+        ctx.enter_context(tc.manual_schedule())
 
-        hid_t, x_t, adj_t = {}, {}, {}
-        hid_g, hid_q, h_g, h_q, v_q = {}, {}, {}, {}, {}
-        a_g, r_ps = {}, {}
-        count = {"tp": 0}
+        hid_t, x_t, o_t, adj_t = {}, {}, {}, {}
+        hid_g, hid_q, h_g, h_q, v_g, v_q = {}, {}, {}, {}, {}, {}
+        a_g, a_tp, rs_ps, r4, r_ps, w_d = {}, {}, {}, {}, {}, {}
 
         def evacuate(engine, dst, src):
             if engine == "s":
@@ -44,9 +50,9 @@ def tile_akgcn_pb_t_kernel(tc, x, hid, adj, lam_raw, theta, out):
             else:
                 nc.vector.tensor_copy(out=dst, in_=src)
 
-        def quantise(src, name):
-            codes = c_pool.tile([P, 512], U32, name=name + "_c", align_bytes=64)
-            scales = c_pool.tile([P, 512], U8, name=name + "_s", align_bytes=64)
+        def quantise(src, name, bufs):
+            codes = c_pool.tile([P, 512], U32, name=name + "_c", align_bytes=64, bufs=bufs)
+            scales = c_pool.tile([P, 512], U8, name=name + "_s", align_bytes=64, bufs=bufs)
             nc.vector.quantize_mx(out=codes[:].bitcast(FP8X4), scales=scales[:], in_=src)
             return codes, scales
 
@@ -62,7 +68,8 @@ def tile_akgcn_pb_t_kernel(tc, x, hid, adj, lam_raw, theta, out):
             adj_t[b] = v_pool.tile([P, 4 * N], BF16, name="adj_t")
             nc.sync.dma_start(out=adj_t[b][:], in_=adj[b].rearrange("(p i) m -> p (i m)", i=4))
 
-        def word_transposes(words, step, dst_words, engines):
+        def word_transposes(words, step):
+            banks = []
             for half in range(2):
                 tp = tp_pool.tile([P, 2, 2, P], F32, name="tp")
                 for lo in range(2):
@@ -73,27 +80,26 @@ def tile_akgcn_pb_t_kernel(tc, x, hid, adj, lam_raw, theta, out):
                         else:
                             src = words[:, base + u : base + 256 : 2]
                         nc.tensor.transpose(tp[:, lo, u, :], src, ident[:])
+                banks.append(tp)
+            return banks
+
+        def word_evacuations(banks, dst_words, engine):
+            for half in range(2):
                 evacuate(
-                    engines[half],
+                    engine,
                     dst_words[:, half * 512 : (half + 1) * 512].rearrange("q (l p u) -> q l p u", l=2, u=2),
-                    tp[:].rearrange("q l u p -> q l p u"),
+                    banks[half][:].rearrange("q l u p -> q l p u"),
                 )
 
-        def stage_t(j):
-            hid_g[j] = g_pool.tile([P, 4 * N], BF16, name="hid_g", align_bytes=64)
-            engines = []
+        def plane_evacuations(banks, dst_words, engine):
+            planes = dst_words.rearrange("q (u h l p) -> q h l u p", u=2, h=2, l=2)
             for half in range(2):
-                engines.append("v" if count["tp"] % 3 == 2 else "s")
-                count["tp"] += 1
-            word_transposes(hid_t[j][:].bitcast(F32), 1, hid_g[j][:].bitcast(F32), engines)
+                evacuate(engine, planes[:, half], banks[half][:])
 
-        def stage_q1(j):
-            hid_q[j] = quantise(hid_g[j][:], "hid")
 
-        def stage_m1(j):
+        def stage_m1(j, groups):
             codes, scales = hid_q[j]
-            h_g[j] = g_pool.tile([P, C, 4], BF16, name="h_g", align_bytes=64)
-            for s in range(4):
+            for s in groups:
                 cols = slice(s * P, (s + 1) * P)
                 h_ps = h_pool.tile([P, 4, P], F32, name="h_ps")
                 for t in range(4):
@@ -109,13 +115,10 @@ def tile_akgcn_pb_t_kernel(tc, x, hid, adj, lam_raw, theta, out):
                     )
                 evacuate("s", h_g[j][:, cols, :], h_ps[:].rearrange("p t c -> p c t"))
 
-        def stage_q2(j):
-            h_q[j] = quantise(h_g[j][:].rearrange("p c t -> p (c t)"), "h")
-
-        def stage_m2(j, o_t):
+        def stage_m2(j, tiles):
             codes, scales = h_q[j]
             vc, vs = v_q[j // T]
-            for i in range(4):
+            for i in tiles:
                 rows = slice(i * P, (i + 1) * P)
                 z_ps = z_pool.tile([P, C], F32, name="z_ps", tag="z")
                 nc.tensor.matmul_mx(
@@ -127,139 +130,157 @@ def tile_akgcn_pb_t_kernel(tc, x, hid, adj, lam_raw, theta, out):
                     start=True,
                     stop=True,
                 )
-                nc.scalar.activation(out=o_t[:, i * C : (i + 1) * C], in_=z_ps[:], func=ACT.Sigmoid)
+                nc.scalar.activation(out=o_t[j][:, i * C : (i + 1) * C], in_=z_ps[:], func=ACT.Sigmoid)
 
-        def relu_x(j):
-            nc.vector.tensor_scalar_max(out=x_t[j][:], in0=x_t[j][:], scalar1=0.0)
-
-        def finish(j, o_t, pieces):
+        def finish(j, pieces):
             dst = out[j // T, j % T].rearrange("(p i) c -> p (i c)", i=4)
             width = 4 * C // pieces
             for k in range(pieces):
                 cols = slice(k * width, (k + 1) * width)
                 nc.vector.scalar_tensor_tensor(
-                    out=o_t[:, cols], in0=o_t[:, cols], scalar=0.5, in1=x_t[j][:, cols], op0=ALU.max, op1=ALU.add
+                    out=o_t[j][:, cols], in0=o_t[j][:, cols], scalar=0.5, in1=x_t[j][:, cols], op0=ALU.max, op1=ALU.add
                 )
-                nc.sync.dma_start(out=dst[:, cols], in_=o_t[:, cols])
+                nc.sync.dma_start(out=dst[:, cols], in_=o_t[j][:, cols])
 
-        def v_transposes(b):
-            a_g[b] = v_pool.tile([P, VW], BF16, name="a_g", align_bytes=64)
-            word_transposes(adj_t[b][:].bitcast(F32), 2, a_g[b][:, 0 : 4 * N].bitcast(F32), ["s", "s"])
+        def diagonal(tile_ap):
+            return tile_ap[:, 0 : 4 * DIAG].rearrange("p (a c) -> p a c", c=DIAG)[:, :, 0:512:4]
 
-        def v_sums(b):
-            grouped = a_g[b][:, 0 : 4 * N].rearrange("p (n t) -> p n t", t=4)
-            rs_ps = z_pool.tile([P, 4, 32], F32, name="rs_ps", tag="z")
+        def v_row_sums(b):
+            rs_ps[b] = z_pool.tile([P, 4, 32], F32, name="rs_ps", tag="z")
             for i in range(4):
                 for t in range(4):
                     nc.tensor.matmul(
-                        out=rs_ps[:, i, :],
-                        lhsT=grouped[:, i * P : (i + 1) * P, t],
+                        out=rs_ps[b][:, i, :],
+                        lhsT=a_g[b][:, 0 : 4 * N].rearrange("p (u n e) -> p u e n", u=2, e=2)[:, t // 2, t % 2, i * P : (i + 1) * P],
                         rhs=ones[:],
                         start=(t == 0),
                         stop=(t == 3),
                     )
+
+        def v_reciprocals(b):
             s4 = v_pool.tile([P, 4], F32, name="s4")
-            nc.vector.tensor_scalar(out=s4[:], in0=rs_ps[:, :, 0], scalar1=gain[:, 0:1], scalar2=None, op0=ALU.add)
-            r4 = v_pool.tile([P, 4], F32, name="r4")
-            nc.vector.reciprocal(out=r4[:], in_=s4[:])
+            nc.vector.tensor_scalar(out=s4[:], in0=rs_ps[b][:, :, 0], scalar1=gain[:, 0:1], scalar2=None, op0=ALU.add)
+            r4[b] = v_pool.tile([P, 4], F32, name="r4")
+            nc.vector.reciprocal(out=r4[b][:], in_=s4[:])
+
+        def v_spread(b):
             r_ps[b] = z_pool.tile([P, 4, P], F32, name="r_ps", tag="z")
             for i in range(4):
                 nc.tensor.matmul(
                     out=r_ps[b][:, i, :],
-                    lhsT=r4[:, i : i + 1].to_broadcast([P, P]),
+                    lhsT=r4[b][:, i : i + 1].to_broadcast([P, P]),
                     rhs=ident[:],
                     start=True,
                     stop=True,
                 )
 
-        def v_scale(b):
-            v_g = v_pool.tile([P, VW], BF16, name="v_g", align_bytes=64)
-            nc.vector.tensor_tensor(
-                out=v_g[:, 0 : 4 * N].rearrange("p (n t) -> p n t", t=4),
-                in0=a_g[b][:, 0 : 4 * N].rearrange("p (n t) -> p n t", t=4),
-                in1=r_ps[b][:].rearrange("p i n -> p (i n)").unsqueeze(2).to_broadcast([P, N, 4]),
-                op=ALU.mult,
-            )
-            w_d = v_pool.tile([P, 4, P], F32, name="w_d")
-            nc.vector.scalar_tensor_tensor(
-                out=w_d[:],
-                in0=ident[:].unsqueeze(1).to_broadcast([P, 4, P]),
-                scalar=gain[:, 0:1],
-                in1=a_g[b][:, 0 : 4 * DIAG].rearrange("p (a c) -> p a c", c=DIAG)[:, :, 0:512:4],
-                op0=ALU.mult,
-                op1=ALU.add,
-            )
-            nc.vector.tensor_tensor(
-                out=v_g[:, 0 : 4 * DIAG].rearrange("p (a c) -> p a c", c=DIAG)[:, :, 0:512:4],
-                in0=w_d[:],
-                in1=r_ps[b][:],
-                op=ALU.mult,
-            )
-            v_q[b] = quantise(v_g[:, 0 : 4 * N], "v")
+        def v_diag_sum(b):
+            w_d[b] = v_pool.tile([P, 4, P], F32, name="w_d")
+            for a in range(2):
+                nc.vector.scalar_tensor_tensor(
+                    out=w_d[b][:, 2 * a : 2 * a + 2, :],
+                    in0=ident[:].unsqueeze(1).to_broadcast([P, 2, P]),
+                    scalar=gain[:, 0:1],
+                    in1=a_g[b][:, a * 1536 : a * 1536 + 514].rearrange("p (c x) -> p c x", c=2)[:, :, 0:256:2],
+                    op0=ALU.mult,
+                    op1=ALU.add,
+                )
 
+        def v_scale(b):
+            v_g[b] = v_pool.tile([P, VW], BF16, name="v_g", align_bytes=64)
+            nc.vector.tensor_tensor(
+                out=v_g[b][:, 0 : 4 * N].rearrange("p (n u e) -> p n u e", u=2, e=2),
+                in0=a_g[b][:, 0 : 4 * N].rearrange("p (u n e) -> p n u e", u=2, e=2),
+                in1=r_ps[b][:].rearrange("p i n -> p (i n)").unsqueeze(2).unsqueeze(3).to_broadcast([P, N, 2, 2]),
+                op=ALU.mult,
+            )
+
+        def v_finish(b):
+            nc.vector.tensor_tensor(out=diagonal(v_g[b]), in0=w_d[b][:], in1=r_ps[b][:], op=ALU.mult)
+            v_q[b] = quantise(v_g[b][:, 0 : 4 * N], "v", 2)
+
+        def live(j):
+            return 0 <= j < NJ
+
+        lam_b = const.tile([P, 1], BF16, name="lam_b")
+        nc.scalar.dma_start(out=lam_b[:], in_=lam_raw.partition_broadcast(P))
+        load_hid(0)
         th_raw = const.tile([P, 4, C], BF16, name="th_raw")
         nc.sync.dma_start(
             out=th_raw[:].rearrange("q (u e) n -> q u (e n)", u=2),
             in_=theta.rearrange("(u q e) n -> q u (e n)", u=2, e=2),
         )
-        load_hid(0)
         load_adj(0)
-        lam_b = const.tile([P, 1], BF16, name="lam_b")
-        nc.sync.dma_start(out=lam_b[:], in_=lam_raw.partition_broadcast(P))
         load_hid(1)
-        load_x(0)
-        load_hid(2)
-        load_x(1)
-        load_hid(3)
-
         ident = const.tile([P, P], F32, name="ident")
         make_identity(nc, ident[:])
         ones = const.tile([P, 32], BF16, name="ones")
         nc.vector.memset(ones[:], 1.0)
+        warm = const.tile([P, 32], BF16, name="warm")
+        nc.scalar.activation(out=warm[:], in_=ones[:], func=ACT.Sigmoid)
         gain = const.tile([P, 1], F32, name="gain")
         nc.vector.tensor_scalar_max(out=gain[:], in0=lam_b[:], scalar1=0.0)
-
         th_g = const.tile([P, C, 4], BF16, name="th_g", align_bytes=64)
-        nc.vector.tensor_copy(out=th_g[:], in_=th_raw[:].rearrange("q t n -> q n t"))
         th_c = const.tile([P, C], U32, name="th_c", align_bytes=64)
         th_s = const.tile([P, C], U8, name="th_s", align_bytes=64)
 
-        stage_t(0)
-        nc.vector.quantize_mx(
-            out=th_c[:].bitcast(FP8X4), scales=th_s[:], in_=th_g[:].rearrange("q n t -> q (n t)")
-        )
-        v_transposes(0)
-        stage_q1(0)
-        stage_t(1)
-        stage_m1(0)
-        v_sums(0)
-        stage_q1(1)
-        v_scale(0)
-        stage_q2(0)
+        for k in range(FIRST, NJ + 1):
+            parts = {}
+            if 0 <= (k + 4) // T < B:
+                parts[(k + 4) % T] = (k + 4) // T
 
-        for k in range(NJ):
-            b, t = k // T, k % T
-            if k + 4 < NJ:
-                load_hid(k + 4)
-            if k + 2 < NJ:
+            if live(k + LEAD_T + 2):
+                load_hid(k + LEAD_T + 2)
+            if live(k + 2):
                 load_x(k + 2)
-            if t == 0 and b + 1 < B:
-                load_adj(b + 1)
-            if k + 2 < NJ:
-                stage_t(k + 2)
-            if t == 1 and b + 1 < B:
-                v_transposes(b + 1)
-            if k + 1 < NJ:
-                stage_m1(k + 1)
-            o_t = o_pool.tile([P, 4 * C], F32, name="o_t")
-            stage_m2(k, o_t)
-            if t == 1 and b + 1 < B:
-                v_sums(b + 1)
-            relu_x(k)
-            if k + 2 < NJ:
-                stage_q1(k + 2)
-            finish(k, o_t, 4 if k == NJ - 1 else 1)
-            if k + 1 < NJ:
-                stage_q2(k + 1)
-            if t == 2 and b + 1 < B:
-                v_scale(b + 1)
+            if parts.get(1, B) + 1 < B:
+                load_adj(parts[1] + 1)
+
+            if live(k - 1):
+                finish(k - 1, 4 if k >= NJ - 1 else 1)
+            if k == FIRST + 1:
+                nc.vector.tensor_copy(out=th_g[:], in_=th_raw[:].rearrange("q t n -> q n t"))
+                nc.vector.quantize_mx(
+                    out=th_c[:].bitcast(FP8X4), scales=th_s[:], in_=th_g[:].rearrange("q n t -> q (n t)")
+                )
+            if live(k + LEAD_Q):
+                hid_q[k + LEAD_Q] = quantise(hid_g[k + LEAD_Q][:], "hid", 2)
+
+            j = k + LEAD_M
+            if live(j):
+                h_g[j] = g_pool.tile([P, C, 4], BF16, name="h_g", align_bytes=64)
+                stage_m1(j, [0, 1, 2])
+            if 0 in parts:
+                a_tp[parts[0]] = word_transposes(adj_t[parts[0]][:].bitcast(F32), 2)
+            if 1 in parts:
+                v_row_sums(parts[1])
+            if 2 in parts:
+                v_spread(parts[2])
+            if live(j):
+                stage_m1(j, [3])
+            if 0 in parts:
+                a_g[parts[0]] = v_pool.tile([P, VW], BF16, name="a_g")
+                plane_evacuations(a_tp[parts[0]], a_g[parts[0]][:, 0 : 4 * N].bitcast(F32), "s")
+            if live(j):
+                h_q[j] = quantise(h_g[j][:].rearrange("p c t -> p (c t)"), "h", 5)
+
+            if live(k):
+                o_t[k] = o_pool.tile([P, 4 * C], F32, name="o_t")
+                stage_m2(k, [0, 1])
+            jt = k + LEAD_T
+            if live(jt):
+                banks = word_transposes(hid_t[jt][:].bitcast(F32), 1)
+            if live(k):
+                stage_m2(k, [2, 3])
+            if live(k + 1):
+                nc.vector.tensor_scalar_max(out=x_t[k + 1][:], in0=x_t[k + 1][:], scalar1=0.0)
+            if live(jt):
+                hid_g[jt] = g_pool.tile([P, 4 * N], BF16, name="hid_g", align_bytes=64)
+                word_evacuations(banks, hid_g[jt][:].bitcast(F32), "v" if 0 in parts and k >= 0 else "s")
+            if 1 in parts:
+                v_reciprocals(parts[1])
+                v_diag_sum(parts[1])
+            if 2 in parts:
+                v_scale(parts[2])
+            if 3 in parts:
+                v_finish(parts[3])

@@ -23,6 +23,7 @@ LEAD_T = 5
 LEAD_Q = 4
 LEAD_M = 3
 FIRST = -5
+CLOSE = NJ - 3
 
 
 def tile_akgcn_pb_t_kernel(tc, x, hid, adj, lam_raw, theta, out):
@@ -131,16 +132,15 @@ def tile_akgcn_pb_t_kernel(tc, x, hid, adj, lam_raw, theta, out):
                     stop=True,
                 )
                 nc.scalar.activation(out=o_t[j][:, i * C : (i + 1) * C], in_=z_ps[:], func=ACT.Sigmoid)
+                if j >= CLOSE:
+                    finish(j, slice(i * C, (i + 1) * C))
 
-        def finish(j, pieces):
+        def finish(j, cols):
             dst = out[j // T, j % T].rearrange("(p i) c -> p (i c)", i=4)
-            width = 4 * C // pieces
-            for k in range(pieces):
-                cols = slice(k * width, (k + 1) * width)
-                nc.vector.scalar_tensor_tensor(
-                    out=o_t[j][:, cols], in0=o_t[j][:, cols], scalar=0.5, in1=x_t[j][:, cols], op0=ALU.max, op1=ALU.add
-                )
-                nc.sync.dma_start(out=dst[:, cols], in_=o_t[j][:, cols])
+            nc.vector.scalar_tensor_tensor(
+                out=o_t[j][:, cols], in0=o_t[j][:, cols], scalar=0.5, in1=x_t[j][:, cols], op0=ALU.max, op1=ALU.add
+            )
+            nc.sync.dma_start(out=dst[:, cols], in_=o_t[j][:, cols])
 
         def diagonal(tile_ap):
             return tile_ap[:, 0 : 4 * DIAG].rearrange("p (a c) -> p a c", c=DIAG)[:, :, 0:512:4]
@@ -224,7 +224,7 @@ def tile_akgcn_pb_t_kernel(tc, x, hid, adj, lam_raw, theta, out):
         th_c = const.tile([P, C], U32, name="th_c", align_bytes=64)
         th_s = const.tile([P, C], U8, name="th_s", align_bytes=64)
 
-        for k in range(FIRST, NJ + 1):
+        for k in range(FIRST, NJ):
             parts = {}
             if 0 <= (k + 4) // T < B:
                 parts[(k + 4) % T] = (k + 4) // T
@@ -236,8 +236,8 @@ def tile_akgcn_pb_t_kernel(tc, x, hid, adj, lam_raw, theta, out):
             if parts.get(1, B) + 1 < B:
                 load_adj(parts[1] + 1)
 
-            if live(k - 1):
-                finish(k - 1, 4 if k >= NJ - 1 else 1)
+            if 0 <= k - 1 < CLOSE:
+                finish(k - 1, slice(0, 4 * C))
             if k == FIRST + 1:
                 nc.vector.tensor_copy(out=th_g[:], in_=th_raw[:].rearrange("q t n -> q n t"))
                 nc.vector.quantize_mx(

@@ -23,7 +23,7 @@ LEAD_T = 5
 LEAD_Q = 4
 LEAD_M = 3
 FIRST = -5
-CLOSE = NJ - 3
+CLOSE = NJ - 4
 
 
 def tile_akgcn_pb_t_kernel(tc, x, hid, adj, lam_raw, theta, out):
@@ -31,7 +31,7 @@ def tile_akgcn_pb_t_kernel(tc, x, hid, adj, lam_raw, theta, out):
     with ExitStack() as ctx:
         const = ctx.enter_context(tc.tile_pool(name="const", bufs=1))
         hid_pool = ctx.enter_context(tc.tile_pool(name="hid_pool", bufs=4))
-        x_pool = ctx.enter_context(tc.tile_pool(name="x_pool", bufs=5))
+        x_pool = ctx.enter_context(tc.tile_pool(name="x_pool", bufs=10))
         o_pool = ctx.enter_context(tc.tile_pool(name="o_pool", bufs=4))
         g_pool = ctx.enter_context(tc.tile_pool(name="g_pool", bufs=2))
         c_pool = ctx.enter_context(tc.tile_pool(name="c_pool", bufs=3))
@@ -202,6 +202,9 @@ def tile_akgcn_pb_t_kernel(tc, x, hid, adj, lam_raw, theta, out):
         def live(j):
             return 0 <= j < NJ
 
+        def relu_step(j):
+            return max(j - 6, j // 2 - 3)
+
         lam_b = const.tile([P, 1], BF16, name="lam_b")
         nc.scalar.dma_start(out=lam_b[:], in_=lam_raw.partition_broadcast(P))
         load_hid(0)
@@ -231,8 +234,9 @@ def tile_akgcn_pb_t_kernel(tc, x, hid, adj, lam_raw, theta, out):
 
             if live(k + LEAD_T + 2):
                 load_hid(k + LEAD_T + 2)
-            if live(k + 2):
-                load_x(k + 2)
+            for jx in range(NJ):
+                if relu_step(jx) - 2 == k:
+                    load_x(jx)
             if parts.get(1, B) + 1 < B:
                 load_adj(parts[1] + 1)
 
@@ -261,6 +265,9 @@ def tile_akgcn_pb_t_kernel(tc, x, hid, adj, lam_raw, theta, out):
             if 0 in parts:
                 a_g[parts[0]] = v_pool.tile([P, VW], BF16, name="a_g")
                 plane_evacuations(a_tp[parts[0]], a_g[parts[0]][:, 0 : 4 * N].bitcast(F32), "s")
+            for jx in range(NJ):
+                if relu_step(jx) == k:
+                    nc.vector.tensor_scalar_max(out=x_t[jx][:], in0=x_t[jx][:], scalar1=0.0)
             if live(j):
                 h_q[j] = quantise(h_g[j][:].rearrange("p c t -> p (c t)"), "h", 5)
 
@@ -272,8 +279,6 @@ def tile_akgcn_pb_t_kernel(tc, x, hid, adj, lam_raw, theta, out):
                 banks = word_transposes(hid_t[jt][:].bitcast(F32), 1)
             if live(k):
                 stage_m2(k, [2, 3])
-            if live(k + 1):
-                nc.vector.tensor_scalar_max(out=x_t[k + 1][:], in0=x_t[k + 1][:], scalar1=0.0)
             if live(jt):
                 hid_g[jt] = g_pool.tile([P, 4 * N], BF16, name="hid_g", align_bytes=64)
                 word_evacuations(banks, hid_g[jt][:].bitcast(F32), "v" if 0 in parts and k >= 0 else "s")

@@ -36,9 +36,7 @@ def tile_akgcn_pb_t_kernel(tc, x, hid, adj, lam_raw, theta, out):
         g_pool = ctx.enter_context(tc.tile_pool(name="g_pool", bufs=2))
         c_pool = ctx.enter_context(tc.tile_pool(name="c_pool", bufs=3))
         v_pool = ctx.enter_context(tc.tile_pool(name="v_pool", bufs=2))
-        tp_pool = ctx.enter_context(tc.psum_pool(name="tp_pool", bufs=2))
-        h_pool = ctx.enter_context(tc.psum_pool(name="h_pool", bufs=3))
-        z_pool = ctx.enter_context(tc.psum_pool(name="z_pool", bufs=3))
+        ps_pool = ctx.enter_context(tc.psum_pool(name="ps_pool", bufs=8))
         ctx.enter_context(tc.manual_schedule())
 
         hid_t, x_t, o_t, adj_t = {}, {}, {}, {}
@@ -57,22 +55,28 @@ def tile_akgcn_pb_t_kernel(tc, x, hid, adj, lam_raw, theta, out):
             nc.vector.quantize_mx(out=codes[:].bitcast(FP8X4), scales=scales[:], in_=src)
             return codes, scales
 
-        def load_hid(j):
+        def load(tile, source, pieces):
+            width = 4 * C // pieces
+            for i in range(pieces):
+                cols = slice(i * width, (i + 1) * width)
+                nc.sync.dma_start(out=tile[:, cols], in_=source.rearrange("(p i) c -> p (i c)", i=4)[:, cols])
+
+        def load_hid(j, pieces=1):
             hid_t[j] = hid_pool.tile([P, 4 * C], BF16, name="hid_t")
-            nc.sync.dma_start(out=hid_t[j][:], in_=hid[j // T, j % T].rearrange("(p t) c -> p (t c)", t=4))
+            load(hid_t[j], hid[j // T, j % T], pieces)
 
         def load_x(j):
             x_t[j] = x_pool.tile([P, 4 * C], BF16, name="x_t")
             nc.sync.dma_start(out=x_t[j][:], in_=x[j // T, j % T].rearrange("(p i) c -> p (i c)", i=4))
 
-        def load_adj(b):
+        def load_adj(b, pieces=1):
             adj_t[b] = v_pool.tile([P, 4 * N], BF16, name="adj_t")
-            nc.sync.dma_start(out=adj_t[b][:], in_=adj[b].rearrange("(p i) m -> p (i m)", i=4))
+            load(adj_t[b], adj[b], pieces)
 
         def word_transposes(words, step):
             banks = []
             for half in range(2):
-                tp = tp_pool.tile([P, 2, 2, P], F32, name="tp")
+                tp = ps_pool.tile([P, 2, 2, P], F32, name="tp", tag="bank")
                 for lo in range(2):
                     for u in range(2):
                         base = (2 * half + lo) * 256
@@ -84,10 +88,10 @@ def tile_akgcn_pb_t_kernel(tc, x, hid, adj, lam_raw, theta, out):
                 banks.append(tp)
             return banks
 
-        def word_evacuations(banks, dst_words, engine):
+        def word_evacuations(banks, dst_words, engines):
             for half in range(2):
                 evacuate(
-                    engine,
+                    engines[half],
                     dst_words[:, half * 512 : (half + 1) * 512].rearrange("q (l p u) -> q l p u", l=2, u=2),
                     banks[half][:].rearrange("q l u p -> q l p u"),
                 )
@@ -102,7 +106,7 @@ def tile_akgcn_pb_t_kernel(tc, x, hid, adj, lam_raw, theta, out):
             codes, scales = hid_q[j]
             for s in groups:
                 cols = slice(s * P, (s + 1) * P)
-                h_ps = h_pool.tile([P, 4, P], F32, name="h_ps")
+                h_ps = ps_pool.tile([P, 4, P], F32, name="h_ps", tag="bank")
                 for t in range(4):
                     rows = slice(t * P, (t + 1) * P)
                     nc.tensor.matmul_mx(
@@ -121,7 +125,7 @@ def tile_akgcn_pb_t_kernel(tc, x, hid, adj, lam_raw, theta, out):
             vc, vs = v_q[j // T]
             for i in tiles:
                 rows = slice(i * P, (i + 1) * P)
-                z_ps = z_pool.tile([P, C], F32, name="z_ps", tag="z")
+                z_ps = ps_pool.tile([P, C], F32, name="z_ps", tag="bank")
                 nc.tensor.matmul_mx(
                     out=z_ps[:],
                     lhsT=vc[:, rows].bitcast(FP8X4),
@@ -146,7 +150,7 @@ def tile_akgcn_pb_t_kernel(tc, x, hid, adj, lam_raw, theta, out):
             return tile_ap[:, 0 : 4 * DIAG].rearrange("p (a c) -> p a c", c=DIAG)[:, :, 0:512:4]
 
         def v_row_sums(b):
-            rs_ps[b] = z_pool.tile([P, 4, 32], F32, name="rs_ps", tag="z")
+            rs_ps[b] = ps_pool.tile([P, 4, 32], F32, name="rs_ps", tag="bank")
             for i in range(4):
                 for t in range(4):
                     nc.tensor.matmul(
@@ -164,7 +168,7 @@ def tile_akgcn_pb_t_kernel(tc, x, hid, adj, lam_raw, theta, out):
             nc.vector.reciprocal(out=r4[b][:], in_=s4[:])
 
         def v_spread(b):
-            r_ps[b] = z_pool.tile([P, 4, P], F32, name="r_ps", tag="z")
+            r_ps[b] = ps_pool.tile([P, 4, P], F32, name="r_ps", tag="bank")
             for i in range(4):
                 nc.tensor.matmul(
                     out=r_ps[b][:, i, :],
@@ -202,18 +206,21 @@ def tile_akgcn_pb_t_kernel(tc, x, hid, adj, lam_raw, theta, out):
         def live(j):
             return 0 <= j < NJ
 
+        def hid_engines(k):
+            return ("vv", "sv", "ss", "ss")[k % T] if k >= 0 else "ss"
+
         def relu_step(j):
             return max(j - 6, j // 2 - 3)
 
         lam_b = const.tile([P, 1], BF16, name="lam_b")
         nc.scalar.dma_start(out=lam_b[:], in_=lam_raw.partition_broadcast(P))
-        load_hid(0)
+        load_hid(0, 2)
         th_raw = const.tile([P, 4, C], BF16, name="th_raw")
         nc.sync.dma_start(
             out=th_raw[:].rearrange("q (u e) n -> q u (e n)", u=2),
             in_=theta.rearrange("(u q e) n -> q u (e n)", u=2, e=2),
         )
-        load_adj(0)
+        load_adj(0, 2)
         load_hid(1)
         ident = const.tile([P, P], F32, name="ident")
         make_identity(nc, ident[:])
@@ -281,7 +288,7 @@ def tile_akgcn_pb_t_kernel(tc, x, hid, adj, lam_raw, theta, out):
                 stage_m2(k, [2, 3])
             if live(jt):
                 hid_g[jt] = g_pool.tile([P, 4 * N], BF16, name="hid_g", align_bytes=64)
-                word_evacuations(banks, hid_g[jt][:].bitcast(F32), "v" if 0 in parts and k >= 0 else "s")
+                word_evacuations(banks, hid_g[jt][:].bitcast(F32), hid_engines(k))
             if 1 in parts:
                 v_reciprocals(parts[1])
                 v_diag_sum(parts[1])

@@ -31,15 +31,15 @@ def tile_akgcn_pb_t_kernel(tc, x, hid, adj, lam_raw, theta, out):
     with ExitStack() as ctx:
         const = ctx.enter_context(tc.tile_pool(name="const", bufs=1))
         hid_pool = ctx.enter_context(tc.tile_pool(name="hid_pool", bufs=4))
-        x_pool = ctx.enter_context(tc.tile_pool(name="x_pool", bufs=10))
-        o_pool = ctx.enter_context(tc.tile_pool(name="o_pool", bufs=4))
-        g_pool = ctx.enter_context(tc.tile_pool(name="g_pool", bufs=2))
+        x_pool = ctx.enter_context(tc.tile_pool(name="x_pool", bufs=6))
+        o_pool = ctx.enter_context(tc.tile_pool(name="o_pool", bufs=6))
+        g_pool = ctx.enter_context(tc.tile_pool(name="g_pool", bufs=5))
         c_pool = ctx.enter_context(tc.tile_pool(name="c_pool", bufs=3))
         v_pool = ctx.enter_context(tc.tile_pool(name="v_pool", bufs=2))
         ps_pool = ctx.enter_context(tc.psum_pool(name="ps_pool", bufs=8))
         ctx.enter_context(tc.manual_schedule())
 
-        hid_t, x_t, o_t, adj_t = {}, {}, {}, {}
+        hid_t, x_t, x_pair, o_t, adj_t = {}, {}, {}, {}, {}
         hid_g, hid_q, h_g, h_q, v_g, v_q = {}, {}, {}, {}, {}, {}
         a_g, a_tp, rs_ps, r4, r_ps, w_d = {}, {}, {}, {}, {}, {}
 
@@ -66,8 +66,12 @@ def tile_akgcn_pb_t_kernel(tc, x, hid, adj, lam_raw, theta, out):
             load(hid_t[j], hid[j // T, j % T], pieces)
 
         def load_x(j):
-            x_t[j] = x_pool.tile([P, 4 * C], BF16, name="x_t")
-            nc.sync.dma_start(out=x_t[j][:], in_=x[j // T, j % T].rearrange("(p i) c -> p (i c)", i=4))
+            x_pair[j] = x_pool.tile([P, 2, 4 * C], BF16, name="x_pair")
+            nc.sync.dma_start(
+                out=x_pair[j][:], in_=x[j // T, j % T : j % T + 2].rearrange("t (p i) c -> p t (i c)", i=4)
+            )
+            for t in range(2):
+                x_t[j + t] = x_pair[j][:, t, :]
 
         def load_adj(b, pieces=1):
             adj_t[b] = v_pool.tile([P, 4 * N], BF16, name="adj_t")
@@ -158,14 +162,19 @@ def tile_akgcn_pb_t_kernel(tc, x, hid, adj, lam_raw, theta, out):
                         lhsT=a_g[b][:, 0 : 4 * N].rearrange("p (u n e) -> p u e n", u=2, e=2)[:, t // 2, t % 2, i * P : (i + 1) * P],
                         rhs=ones[:],
                         start=(t == 0),
-                        stop=(t == 3),
+                        stop=False,
                     )
+                nc.tensor.matmul(
+                    out=rs_ps[b][:, i, :],
+                    lhsT=ident_b[:],
+                    rhs=gain_b[:, 0:1].to_broadcast([P, 32]),
+                    start=False,
+                    stop=True,
+                )
 
         def v_reciprocals(b):
-            s4 = v_pool.tile([P, 4], F32, name="s4")
-            nc.vector.tensor_scalar(out=s4[:], in0=rs_ps[b][:, :, 0], scalar1=gain[:, 0:1], scalar2=None, op0=ALU.add)
             r4[b] = v_pool.tile([P, 4], F32, name="r4")
-            nc.vector.reciprocal(out=r4[b][:], in_=s4[:])
+            nc.vector.reciprocal(out=r4[b][:], in_=rs_ps[b][:, :, 0])
 
         def v_spread(b):
             r_ps[b] = ps_pool.tile([P, 4, P], F32, name="r_ps", tag="bank")
@@ -224,12 +233,16 @@ def tile_akgcn_pb_t_kernel(tc, x, hid, adj, lam_raw, theta, out):
         load_hid(1)
         ident = const.tile([P, P], F32, name="ident")
         make_identity(nc, ident[:])
+        ident_b = const.tile([P, P], BF16, name="ident_b")
+        make_identity(nc, ident_b[:])
         ones = const.tile([P, 32], BF16, name="ones")
         nc.vector.memset(ones[:], 1.0)
         warm = const.tile([P, 32], BF16, name="warm")
         nc.scalar.activation(out=warm[:], in_=ones[:], func=ACT.Sigmoid)
         gain = const.tile([P, 1], F32, name="gain")
         nc.vector.tensor_scalar_max(out=gain[:], in0=lam_b[:], scalar1=0.0)
+        gain_b = const.tile([P, 1], BF16, name="gain_b")
+        nc.vector.tensor_scalar_max(out=gain_b[:], in0=lam_b[:], scalar1=0.0)
         th_g = const.tile([P, C, 4], BF16, name="th_g", align_bytes=64)
         th_c = const.tile([P, C], U32, name="th_c", align_bytes=64)
         th_s = const.tile([P, C], U8, name="th_s", align_bytes=64)
@@ -241,7 +254,7 @@ def tile_akgcn_pb_t_kernel(tc, x, hid, adj, lam_raw, theta, out):
 
             if live(k + LEAD_T + 2):
                 load_hid(k + LEAD_T + 2)
-            for jx in range(NJ):
+            for jx in range(0, NJ, 2):
                 if relu_step(jx) - 2 == k:
                     load_x(jx)
             if parts.get(1, B) + 1 < B:
@@ -255,7 +268,7 @@ def tile_akgcn_pb_t_kernel(tc, x, hid, adj, lam_raw, theta, out):
                     out=th_c[:].bitcast(FP8X4), scales=th_s[:], in_=th_g[:].rearrange("q n t -> q (n t)")
                 )
             if live(k + LEAD_Q):
-                hid_q[k + LEAD_Q] = quantise(hid_g[k + LEAD_Q][:], "hid", 2)
+                hid_q[k + LEAD_Q] = quantise(hid_g[k + LEAD_Q][:], "hid", 4)
 
             j = k + LEAD_M
             if live(j):
@@ -272,9 +285,9 @@ def tile_akgcn_pb_t_kernel(tc, x, hid, adj, lam_raw, theta, out):
             if 0 in parts:
                 a_g[parts[0]] = v_pool.tile([P, VW], BF16, name="a_g")
                 plane_evacuations(a_tp[parts[0]], a_g[parts[0]][:, 0 : 4 * N].bitcast(F32), "s")
-            for jx in range(NJ):
+            for jx in range(0, NJ, 2):
                 if relu_step(jx) == k:
-                    nc.vector.tensor_scalar_max(out=x_t[jx][:], in0=x_t[jx][:], scalar1=0.0)
+                    nc.vector.tensor_scalar_max(out=x_pair[jx][:], in0=x_pair[jx][:], scalar1=0.0)
             if live(j):
                 h_q[j] = quantise(h_g[j][:].rearrange("p c t -> p (c t)"), "h", 5)
 
@@ -287,7 +300,7 @@ def tile_akgcn_pb_t_kernel(tc, x, hid, adj, lam_raw, theta, out):
             if live(k):
                 stage_m2(k, [2, 3])
             if live(jt):
-                hid_g[jt] = g_pool.tile([P, 4 * N], BF16, name="hid_g", align_bytes=64)
+                hid_g[jt] = g_pool.tile([P, 4 * N], BF16, name="hid_g", align_bytes=64, bufs=4)
                 word_evacuations(banks, hid_g[jt][:].bitcast(F32), hid_engines(k))
             if 1 in parts:
                 v_reciprocals(parts[1])

@@ -140,8 +140,10 @@ def tile_akgcn_pb_t_kernel(tc, x, hid, adj, lam_raw, theta, out):
                     stop=True,
                 )
                 nc.scalar.activation(out=o_t[j][:, i * C : (i + 1) * C], in_=z_ps[:], func=ACT.Sigmoid)
-                if j >= CLOSE:
+                if j == NJ - 1:
                     finish(j, slice(i * C, (i + 1) * C))
+            if CLOSE <= j < NJ - 1:
+                finish(j, slice(tiles[0] * C, (tiles[-1] + 1) * C))
 
         def finish(j, cols):
             dst = out[j // T, j % T].rearrange("(p i) c -> p (i c)", i=4)
@@ -208,15 +210,17 @@ def tile_akgcn_pb_t_kernel(tc, x, hid, adj, lam_raw, theta, out):
                 op=ALU.mult,
             )
 
-        def v_finish(b):
+        def v_diagonal(b):
             nc.vector.tensor_tensor(out=diagonal(v_g[b]), in0=w_d[b][:], in1=r_ps[b][:], op=ALU.mult)
+
+        def v_quantise(b):
             v_q[b] = quantise(v_g[b][:, 0 : 4 * N], "v", 2)
 
         def live(j):
             return 0 <= j < NJ
 
         def hid_engines(k):
-            return ("vv", "sv", "ss", "ss")[k % T] if k >= 0 else "ss"
+            return "vv" if k >= 0 and k % T == 0 else "ss"
 
         def relu_step(j):
             return max(j - 6, j // 2 - 3)
@@ -264,11 +268,14 @@ def tile_akgcn_pb_t_kernel(tc, x, hid, adj, lam_raw, theta, out):
                 finish(k - 1, slice(0, 4 * C))
             if k == FIRST + 1:
                 nc.vector.tensor_copy(out=th_g[:], in_=th_raw[:].rearrange("q t n -> q n t"))
+            if live(k + LEAD_Q):
+                hid_q[k + LEAD_Q] = quantise(hid_g[k + LEAD_Q][:], "hid", 4)
+            if k == FIRST + 1:
                 nc.vector.quantize_mx(
                     out=th_c[:].bitcast(FP8X4), scales=th_s[:], in_=th_g[:].rearrange("q n t -> q (n t)")
                 )
-            if live(k + LEAD_Q):
-                hid_q[k + LEAD_Q] = quantise(hid_g[k + LEAD_Q][:], "hid", 4)
+            if 3 in parts:
+                v_diagonal(parts[3])
 
             j = k + LEAD_M
             if live(j):
@@ -288,6 +295,8 @@ def tile_akgcn_pb_t_kernel(tc, x, hid, adj, lam_raw, theta, out):
             for jx in range(0, NJ, 2):
                 if relu_step(jx) == k:
                     nc.vector.tensor_scalar_max(out=x_pair[jx][:], in0=x_pair[jx][:], scalar1=0.0)
+            if 3 in parts:
+                v_quantise(parts[3])
             if live(j):
                 h_q[j] = quantise(h_g[j][:].rearrange("p c t -> p (c t)"), "h", 5)
 
@@ -307,5 +316,3 @@ def tile_akgcn_pb_t_kernel(tc, x, hid, adj, lam_raw, theta, out):
                 v_diag_sum(parts[1])
             if 2 in parts:
                 v_scale(parts[2])
-            if 3 in parts:
-                v_finish(parts[3])

@@ -23,7 +23,7 @@ LEAD_T = 5
 LEAD_Q = 4
 LEAD_M = 3
 FIRST = -5
-CLOSE = NJ - 4
+CLOSE = NJ - 5
 
 
 def tile_akgcn_pb_t_kernel(tc, x, hid, adj, lam_raw, theta, out):
@@ -295,6 +295,11 @@ def tile_akgcn_pb_t_kernel(tc, x, hid, adj, lam_raw, theta, out):
             for jx in range(0, NJ, 2):
                 if relu_step(jx) == k:
                     nc.vector.tensor_scalar_max(out=x_pair[jx][:], in0=x_pair[jx][:], scalar1=0.0)
+            if 1 in parts:
+                v_reciprocals(parts[1])
+                v_diag_sum(parts[1])
+            if 2 in parts:
+                v_scale(parts[2])
             if 3 in parts:
                 v_quantise(parts[3])
             if live(j):
@@ -311,8 +316,3 @@ def tile_akgcn_pb_t_kernel(tc, x, hid, adj, lam_raw, theta, out):
             if live(jt):
                 hid_g[jt] = g_pool.tile([P, 4 * N], BF16, name="hid_g", align_bytes=64, bufs=4)
                 word_evacuations(banks, hid_g[jt][:].bitcast(F32), hid_engines(k))
-            if 1 in parts:
-                v_reciprocals(parts[1])
-                v_diag_sum(parts[1])
-            if 2 in parts:
-                v_scale(parts[2])

@@ -281,8 +281,6 @@ def tile_akgcn_pb_t_kernel(tc, x, hid, adj, lam_raw, theta, out):
             if live(j):
                 h_g[j] = g_pool.tile([P, C, 4], BF16, name="h_g", align_bytes=64)
                 stage_m1(j, [0, 1, 2])
-            if 0 in parts:
-                a_tp[parts[0]] = word_transposes(adj_t[parts[0]][:].bitcast(F32), 2)
             if 1 in parts:
                 v_row_sums(parts[1])
             if 2 in parts:
@@ -290,6 +288,7 @@ def tile_akgcn_pb_t_kernel(tc, x, hid, adj, lam_raw, theta, out):
             if live(j):
                 stage_m1(j, [3])
             if 0 in parts:
+                a_tp[parts[0]] = word_transposes(adj_t[parts[0]][:].bitcast(F32), 2)
                 a_g[parts[0]] = v_pool.tile([P, VW], BF16, name="a_g")
                 plane_evacuations(a_tp[parts[0]], a_g[parts[0]][:, 0 : 4 * N].bitcast(F32), "s")
             for jx in range(0, NJ, 2):
@@ -300,10 +299,10 @@ def tile_akgcn_pb_t_kernel(tc, x, hid, adj, lam_raw, theta, out):
                 v_diag_sum(parts[1])
             if 2 in parts:
                 v_scale(parts[2])
-            if 3 in parts:
-                v_quantise(parts[3])
             if live(j):
                 h_q[j] = quantise(h_g[j][:].rearrange("p c t -> p (c t)"), "h", 5)
+            if 3 in parts:
+                v_quantise(parts[3])
 
             if live(k):
                 o_t[k] = o_pool.tile([P, 4 * C], F32, name="o_t")

from contextlib import ExitStack

import concourse.mybir as mybir
from concourse.masks import make_identity

F32 = mybir.dt.float32
BF16 = mybir.dt.bfloat16
U32 = mybir.dt.uint32
U8 = mybir.dt.uint8
FP8X4 = mybir.dt.float8_e4m3fn_x4
ALU = mybir.AluOpType
ACT = mybir.ActivationFunctionType

B, T, N, C = 4, 4, 512, 512
P = 128
NJ = B * T
FLOPS = 2 * B * T * N * C * C + 2 * B * T * N * N * C
DIAG = 513
VW = 2112


LEAD_T = 5
LEAD_Q = 4
LEAD_M = 3
FIRST = -5
CLOSE = NJ - 5


def tile_akgcn_pb_t_kernel(tc, x, hid, adj, lam_raw, theta, out):
    nc = tc.nc
    with ExitStack() as ctx:
        const = ctx.enter_context(tc.tile_pool(name="const", bufs=1))
        hid_pool = ctx.enter_context(tc.tile_pool(name="hid_pool", bufs=4))
        x_pool = ctx.enter_context(tc.tile_pool(name="x_pool", bufs=6))
        o_pool = ctx.enter_context(tc.tile_pool(name="o_pool", bufs=6))
        g_pool = ctx.enter_context(tc.tile_pool(name="g_pool", bufs=5))
        c_pool = ctx.enter_context(tc.tile_pool(name="c_pool", bufs=3))
        v_pool = ctx.enter_context(tc.tile_pool(name="v_pool", bufs=2))
        ps_pool = ctx.enter_context(tc.psum_pool(name="ps_pool", bufs=8))
        ctx.enter_context(tc.manual_schedule())

        hid_t, x_t, x_pair, o_t, adj_t = {}, {}, {}, {}, {}
        hid_g, hid_q, h_g, h_q, v_g, v_q = {}, {}, {}, {}, {}, {}
        a_g, a_tp, rs_ps, r4, r_ps, w_d = {}, {}, {}, {}, {}, {}

        def evacuate(engine, dst, src):
            if engine == "s":
                nc.scalar.copy(out=dst, in_=src)
            else:
                nc.vector.tensor_copy(out=dst, in_=src)

        def quantise(src, name, bufs):
            codes = c_pool.tile([P, 512], U32, name=name + "_c", align_bytes=64, bufs=bufs)
            scales = c_pool.tile([P, 512], U8, name=name + "_s", align_bytes=64, bufs=bufs)
            nc.vector.quantize_mx(out=codes[:].bitcast(FP8X4), scales=scales[:], in_=src)
            return codes, scales

        def load(tile, source, pieces):
            width = 4 * C // pieces
            for i in range(pieces):
                cols = slice(i * width, (i + 1) * width)
                nc.sync.dma_start(out=tile[:, cols], in_=source.rearrange("(p i) c -> p (i c)", i=4)[:, cols])

        def load_hid(j, pieces=1):
            hid_t[j] = hid_pool.tile([P, 4 * C], BF16, name="hid_t")
            load(hid_t[j], hid[j // T, j % T], pieces)

        def load_x(j):
            x_pair[j] = x_pool.tile([P, 2, 4 * C], BF16, name="x_pair")
            nc.sync.dma_start(
                out=x_pair[j][:], in_=x[j // T, j % T : j % T + 2].rearrange("t (p i) c -> p t (i c)", i=4)
            )
            for t in range(2):
                x_t[j + t] = x_pair[j][:, t, :]

        def load_adj(b, pieces=1):
            adj_t[b] = v_pool.tile([P, 4 * N], BF16, name="adj_t")
            load(adj_t[b], adj[b], pieces)

        def word_transposes(words, step):
            banks = []
            for half in range(2):
                tp = ps_pool.tile([P, 2, 2, P], F32, name="tp", tag="bank")
                for lo in range(2):
                    for u in range(2):
                        base = (2 * half + lo) * 256
                        if step == 1:
                            src = words[:, base + u * P : base + (u + 1) * P]
                        else:
                            src = words[:, base + u : base + 256 : 2]
                        nc.tensor.transpose(tp[:, lo, u, :], src, ident[:])
                banks.append(tp)
            return banks

        def word_evacuations(banks, dst_words, engines):
            for half in range(2):
                evacuate(
                    engines[half],
                    dst_words[:, half * 512 : (half + 1) * 512].rearrange("q (l p u) -> q l p u", l=2, u=2),
                    banks[half][:].rearrange("q l u p -> q l p u"),
                )

        def plane_evacuations(banks, dst_words, engine):
            planes = dst_words.rearrange("q (u h l p) -> q h l u p", u=2, h=2, l=2)
            for half in range(2):
                evacuate(engine, planes[:, half], banks[half][:])


        def stage_m1(j, groups):
            codes, scales = hid_q[j]
            for s in groups:
                cols = slice(s * P, (s + 1) * P)
                h_ps = ps_pool.tile([P, 4, P], F32, name="h_ps", tag="bank")
                for t in range(4):
                    rows = slice(t * P, (t + 1) * P)
                    nc.tensor.matmul_mx(
                        out=h_ps[:, t, :],
                        lhsT=codes[:, rows].bitcast(FP8X4),
                        lhsT_scale=scales[:, rows],
                        rhs=th_c[:, cols].bitcast(FP8X4),
                        rhs_scale=th_s[:, cols],
                        start=True,
                        stop=True,
                    )
                evacuate("s", h_g[j][:, cols, :], h_ps[:].rearrange("p t c -> p c t"))

        def stage_m2(j, tiles):
            codes, scales = h_q[j]
            vc, vs = v_q[j // T]
            for i in tiles:
                rows = slice(i * P, (i + 1) * P)
                z_ps = ps_pool.tile([P, C], F32, name="z_ps", tag="bank")
                nc.tensor.matmul_mx(
                    out=z_ps[:],
                    lhsT=vc[:, rows].bitcast(FP8X4),
                    lhsT_scale=vs[:, rows],
                    rhs=codes[:].bitcast(FP8X4),
                    rhs_scale=scales[:],
                    start=True,
                    stop=True,
                )
                nc.scalar.activation(out=o_t[j][:, i * C : (i + 1) * C], in_=z_ps[:], func=ACT.Sigmoid)
                if j == NJ - 1:
                    finish(j, slice(i * C, (i + 1) * C))
            if CLOSE <= j < NJ - 1:
                finish(j, slice(tiles[0] * C, (tiles[-1] + 1) * C))

        def finish(j, cols):
            dst = out[j // T, j % T].rearrange("(p i) c -> p (i c)", i=4)
            nc.vector.scalar_tensor_tensor(
                out=o_t[j][:, cols], in0=o_t[j][:, cols], scalar=0.5, in1=x_t[j][:, cols], op0=ALU.max, op1=ALU.add
            )
            nc.sync.dma_start(out=dst[:, cols], in_=o_t[j][:, cols])

        def diagonal(tile_ap):
            return tile_ap[:, 0 : 4 * DIAG].rearrange("p (a c) -> p a c", c=DIAG)[:, :, 0:512:4]

        def v_row_sums(b):
            rs_ps[b] = ps_pool.tile([P, 4, 32], F32, name="rs_ps", tag="bank")
            for i in range(4):
                for t in range(4):
                    nc.tensor.matmul(
                        out=rs_ps[b][:, i, :],
                        lhsT=a_g[b][:, 0 : 4 * N].rearrange("p (u n e) -> p u e n", u=2, e=2)[:, t // 2, t % 2, i * P : (i + 1) * P],
                        rhs=ones[:],
                        start=(t == 0),
                        stop=False,
                    )
                nc.tensor.matmul(
                    out=rs_ps[b][:, i, :],
                    lhsT=ident_b[:],
                    rhs=gain_b[:, 0:1].to_broadcast([P, 32]),
                    start=False,
                    stop=True,
                )

        def v_reciprocals(b):
            r4[b] = v_pool.tile([P, 4], F32, name="r4")
            nc.vector.reciprocal(out=r4[b][:], in_=rs_ps[b][:, :, 0])

        def v_spread(b):
            r_ps[b] = ps_pool.tile([P, 4, P], F32, name="r_ps", tag="bank")
            for i in range(4):
                nc.tensor.matmul(
                    out=r_ps[b][:, i, :],
                    lhsT=r4[b][:, i : i + 1].to_broadcast([P, P]),
                    rhs=ident[:],
                    start=True,
                    stop=True,
                )

        def v_diag_sum(b):
            w_d[b] = v_pool.tile([P, 4, P], F32, name="w_d")
            for a in range(2):
                nc.vector.scalar_tensor_tensor(
                    out=w_d[b][:, 2 * a : 2 * a + 2, :],
                    in0=ident[:].unsqueeze(1).to_broadcast([P, 2, P]),
                    scalar=gain[:, 0:1],
                    in1=a_g[b][:, a * 1536 : a * 1536 + 514].rearrange("p (c x) -> p c x", c=2)[:, :, 0:256:2],
                    op0=ALU.mult,
                    op1=ALU.add,
                )

        def v_scale(b):
            v_g[b] = v_pool.tile([P, VW], BF16, name="v_g", align_bytes=64)
            nc.vector.tensor_tensor(
                out=v_g[b][:, 0 : 4 * N].rearrange("p (n u e) -> p n u e", u=2, e=2),
                in0=a_g[b][:, 0 : 4 * N].rearrange("p (u n e) -> p n u e", u=2, e=2),
                in1=r_ps[b][:].rearrange("p i n -> p (i n)").unsqueeze(2).unsqueeze(3).to_broadcast([P, N, 2, 2]),
                op=ALU.mult,
            )

        def v_diagonal(b):
            nc.vector.tensor_tensor(out=diagonal(v_g[b]), in0=w_d[b][:], in1=r_ps[b][:], op=ALU.mult)

        def v_quantise(b):
            v_q[b] = quantise(v_g[b][:, 0 : 4 * N], "v", 2)

        def live(j):
            return 0 <= j < NJ

        def hid_engines(k):
            return "vv" if k >= 0 and k % T == 0 else "ss"

        def relu_step(j):
            return max(j - 6, j // 2 - 3)

        lam_b = const.tile([P, 1], BF16, name="lam_b")
        nc.scalar.dma_start(out=lam_b[:], in_=lam_raw.partition_broadcast(P))
        load_hid(0, 2)
        th_raw = const.tile([P, 4, C], BF16, name="th_raw")
        nc.sync.dma_start(
            out=th_raw[:].rearrange("q (u e) n -> q u (e n)", u=2),
            in_=theta.rearrange("(u q e) n -> q u (e n)", u=2, e=2),
        )
        load_adj(0, 2)
        load_hid(1)
        ident = const.tile([P, P], F32, name="ident")
        make_identity(nc, ident[:])
        ident_b = const.tile([P, P], BF16, name="ident_b")
        make_identity(nc, ident_b[:])
        ones = const.tile([P, 32], BF16, name="ones")
        nc.vector.memset(ones[:], 1.0)
        warm = const.tile([P, 32], BF16, name="warm")
        nc.scalar.activation(out=warm[:], in_=ones[:], func=ACT.Sigmoid)
        gain = const.tile([P, 1], F32, name="gain")
        nc.vector.tensor_scalar_max(out=gain[:], in0=lam_b[:], scalar1=0.0)
        gain_b = const.tile([P, 1], BF16, name="gain_b")
        nc.vector.tensor_scalar_max(out=gain_b[:], in0=lam_b[:], scalar1=0.0)
        th_g = const.tile([P, C, 4], BF16, name="th_g", align_bytes=64)
        th_c = const.tile([P, C], U32, name="th_c", align_bytes=64)
        th_s = const.tile([P, C], U8, name="th_s", align_bytes=64)

        for k in range(FIRST, NJ):
            parts = {}
            if 0 <= (k + 4) // T < B:
                parts[(k + 4) % T] = (k + 4) // T

            if live(k + LEAD_T + 2):
                load_hid(k + LEAD_T + 2)
            for jx in range(0, NJ, 2):
                if relu_step(jx) - 2 == k:
                    load_x(jx)
            if parts.get(1, B) + 1 < B:
                load_adj(parts[1] + 1)

            if 0 <= k - 1 < CLOSE:
                finish(k - 1, slice(0, 4 * C))
            if k == FIRST + 1:
                nc.vector.tensor_copy(out=th_g[:], in_=th_raw[:].rearrange("q t n -> q n t"))
            if live(k + LEAD_Q):
                hid_q[k + LEAD_Q] = quantise(hid_g[k + LEAD_Q][:], "hid", 4)
            if k == FIRST + 1:
                nc.vector.quantize_mx(
                    out=th_c[:].bitcast(FP8X4), scales=th_s[:], in_=th_g[:].rearrange("q n t -> q (n t)")
                )
            if 3 in parts:
                v_diagonal(parts[3])

            j = k + LEAD_M
            if live(j):
                h_g[j] = g_pool.tile([P, C, 4], BF16, name="h_g", align_bytes=64)
                stage_m1(j, [0, 1, 2])
            if 1 in parts:
                v_row_sums(parts[1])
            if 2 in parts:
                v_spread(parts[2])
            if live(j):
                stage_m1(j, [3])
            if 0 in parts:
                a_tp[parts[0]] = word_transposes(adj_t[parts[0]][:].bitcast(F32), 2)
                a_g[parts[0]] = v_pool.tile([P, VW], BF16, name="a_g")
                plane_evacuations(a_tp[parts[0]], a_g[parts[0]][:, 0 : 4 * N].bitcast(F32), "s")
            for jx in range(0, NJ, 2):
                if relu_step(jx) == k:
                    nc.vector.tensor_scalar_max(out=x_pair[jx][:], in0=x_pair[jx][:], scalar1=0.0)
            if 1 in parts:
                v_reciprocals(parts[1])
                v_diag_sum(parts[1])
            if 2 in parts:
                v_scale(parts[2])
            if live(j):
                h_q[j] = quantise(h_g[j][:].rearrange("p c t -> p (c t)"), "h", 5)
            if 3 in parts:
                v_quantise(parts[3])

            if live(k):
                o_t[k] = o_pool.tile([P, 4 * C], F32, name="o_t")
                stage_m2(k, [0, 1])
            jt = k + LEAD_T
            if live(jt):
                banks = word_transposes(hid_t[jt][:].bitcast(F32), 1)
            if live(k):
                stage_m2(k, [2, 3])
            if live(jt):
                hid_g[jt] = g_pool.tile([P, 4 * N], BF16, name="hid_g", align_bytes=64, bufs=4)
                word_evacuations(banks, hid_g[jt][:].bitcast(F32), hid_engines(k))
